import numpy as np
import ml_dtypes


def mxq(x, axis, fmt="e4m3"):
    dtype, down = {"e4m3": (ml_dtypes.float8_e4m3fn, 7), "e5m2": (ml_dtypes.float8_e5m2, 14)}[fmt]
    v = np.moveaxis(np.asarray(x, np.float32).astype(ml_dtypes.bfloat16).astype(np.float64), axis, -1)
    blocks = v.reshape(v.shape[:-1] + (-1, 32))
    amax = np.abs(blocks).max(-1, keepdims=True)
    byte = np.maximum(np.where(amax > 0, np.frexp(amax)[1] - 1 + 127, 0) - down, 1)
    scale = np.exp2(byte - 127.0)
    codes = (blocks / scale).astype(np.float32).astype(dtype).astype(np.float64)
    return np.moveaxis((codes * scale).reshape(v.shape), -1, axis)


WIDE = False


def mx_kscale(k):
    if not WIDE:
        return np.ones(k)
    levels = np.array([10, -10, 5, -5, 0])
    a = np.random.permutation(np.resize(levels, k // 512 * 4)).reshape(k // 512, 4)
    idx = np.arange(k)
    return np.exp2(a[idx // 512, idx % 128 // 32])


BF16 = ml_dtypes.bfloat16


def bf(x):
    return np.asarray(x, np.float32).astype(BF16)


def f64(x):
    return np.asarray(x).astype(np.float64)


B, DH, DO, L = 128, 256, 1024, 128


def setup_inputs():
    s = mx_kscale(2 * DH)
    t = mx_kscale(DO)
    return {"sbj_vec": bf(np.random.standard_normal((B, DH)) * s[:DH]),
            "obj_vec": bf(np.random.standard_normal((B, DH)) * s[DH:]),
            "W1": bf(np.random.standard_normal((2 * DH, DO)) * 1.28 / np.sqrt(2 * DH) / s[:, None] * t),
            "b1": bf(np.random.standard_normal(DO) * 0.1 * t),
            "W2": bf(np.random.standard_normal((DO, DO)) * 12.0 / DO / t[:, None]),
            "b2": bf(np.random.standard_normal(DO) * 0.1),
            "label_vecs": bf(np.random.standard_normal((L, DO)) * 8.0 / np.sqrt(DO))}


def reference(sbj_vec, obj_vec, W1, b1, W2, b2, label_vecs):
    x = np.concatenate([f64(sbj_vec), f64(obj_vec)], axis=1)
    hidden = (mxq(np.maximum(x, 0.0), 1, "e4m3") @ mxq(f64(W1), 0, "e4m3")) + f64(b1)
    emb = (mxq(np.maximum(hidden, 0.0), 1, "e4m3") @ mxq(f64(W2), 0, "e4m3")) + f64(b2)
    lab = f64(label_vecs)
    scores = np.empty((emb.shape[0], lab.shape[0]))
    for l in range(lab.shape[0]):
        diff = np.maximum(lab[l][None, :] - emb, 0.0)
        scores[:, l] = -np.sqrt(np.sum(diff * diff, axis=1))
    return scores

@@ -1,0 +1,281 @@
+from contextlib import ExitStack
+
+import concourse.mybir as mybir
+from concourse.masks import make_identity
+
+BF16 = mybir.dt.bfloat16
+F32 = mybir.dt.float32
+U32 = mybir.dt.uint32
+U8 = mybir.dt.uint8
+FP8X4 = mybir.dt.float8_e4m3fn_x4
+ALU = mybir.AluOpType
+ACT = mybir.ActivationFunctionType
+
+P = 128
+PACK = 4
+K_PASS = P * PACK
+B, DH, DO, L = 128, 256, 1024, 128
+K1 = 2 * DH
+PASSES2 = DO // K_PASS
+CHUNKS = DO // P
+BANK = 512
+CHUNKS_PER_BANK = BANK // P
+HALVES = CHUNKS // CHUNKS_PER_BANK
+RUN = 4
+SECOND_WAY_LABELS = 22
+FIRST_WAY_LABELS = L - SECOND_WAY_LABELS
+LABELS_PER_BROADCAST = 2
+SQRT_GUARD = 1e-30
+
+FLOPS = 2 * B * K1 * DO + 2 * B * DO * DO + 4 * B * L * DO
+
+
+def regroup_weights(nc, stage, raw):
+    grouped = stage.tile([P, BANK, PACK], BF16, align_bytes=64)
+    dst = grouped[:].rearrange("p (c i) t -> p c t i", i=RUN)
+    src = raw.rearrange("p t (c i) -> p c t i", i=RUN)
+    runs = BANK // RUN
+    nc.vector.tensor_copy(out=dst[:, 0 : runs // 2], in_=src[:, 0 : runs // 2])
+    nc.scalar.copy(out=dst[:, runs // 2 : runs], in_=src[:, runs // 2 : runs])
+    return grouped
+
+
+def quantise(nc, grouped, codes, scales):
+    nc.vector.quantize_mx(out=codes.bitcast(FP8X4), scales=scales, in_=grouped.rearrange("p n t -> p (n t)"))
+
+
+def tile_relationembedding_s_kernel(tc, sbj_vec, obj_vec, W1, b1, W2, b2, label_vecs, out):
+    nc = tc.nc
+    with ExitStack() as ctx:
+        ctx.enter_context(tc.manual_schedule())
+        keep = ctx.enter_context(tc.tile_pool(name="keep", bufs=1))
+        stage = ctx.enter_context(tc.tile_pool(name="stage", bufs=3))
+        work = ctx.enter_context(tc.tile_pool(name="work", bufs=6))
+        wide = ctx.enter_context(tc.tile_pool(name="wide", bufs=2))
+        setup_psum = ctx.enter_context(tc.psum_pool(name="setup_psum", bufs=3))
+        score_psum = ctx.enter_context(tc.psum_pool(name="score_psum", bufs=5))
+
+        x_sb = keep.tile([P, K1], BF16)
+        nc.sync.dma_start(out=x_sb[:, 0:DH], in_=sbj_vec)
+        nc.sync.dma_start(out=x_sb[:, DH:K1], in_=obj_vec)
+        bias_rows = keep.tile([P, P], BF16)
+        nc.vector.memset(bias_rows[:], 0.0)
+        nc.sync.dma_start(out=bias_rows[0:CHUNKS, :], in_=b1.rearrange("(m p) -> m p", p=P))
+        nc.sync.dma_start(out=bias_rows[CHUNKS : 2 * CHUNKS, :], in_=b2.rearrange("(m p) -> m p", p=P))
+        w1_raw = keep.tile([P, PACK, DO], BF16)
+        w1_view = W1.rearrange("(t p) n -> p t n", p=P)
+        for half in range(HALVES):
+            cols = slice(half * BANK, (half + 1) * BANK)
+            nc.sync.dma_start(out=w1_raw[:, :, cols], in_=w1_view[:, :, cols])
+        w2_raw = keep.tile([P, PASSES2, PACK, DO], BF16)
+        w2_view = W2.rearrange("(g t p) n -> p g t n", t=PACK, p=P)
+        for half in range(HALVES):
+            cols = slice(half * BANK, (half + 1) * BANK)
+            for g in range(PASSES2):
+                nc.sync.dma_start(out=w2_raw[:, g, :, cols], in_=w2_view[:, g, :, cols])
+        label_sb = keep.tile([P, DO], BF16)
+        nc.sync.dma_start(out=label_sb[:], in_=label_vecs)
+        label_bcast = keep.tile([P, SECOND_WAY_LABELS, DO], BF16)
+        for i0 in range(0, SECOND_WAY_LABELS, LABELS_PER_BROADCAST):
+            own_rows = label_vecs[FIRST_WAY_LABELS + i0 : FIRST_WAY_LABELS + i0 + LABELS_PER_BROADCAST, :]
+            nc.sync.dma_start(
+                out=label_bcast[:, i0 : i0 + LABELS_PER_BROADCAST, :].rearrange("p l d -> p (l d)"),
+                in_=own_rows.rearrange("l d -> (l d)").partition_broadcast(P),
+            )
+
+        ident_bf = keep.tile([P, P], BF16)
+        make_identity(nc, ident_bf[:])
+        ident_f32 = keep.tile([P, P], F32)
+        make_identity(nc, ident_f32[:])
+        one = keep.tile([P, 1], F32)
+        nc.vector.memset(one[:], 1.0)
+        nc.scalar.sqrt(out=one[:], in_=one[:])
+
+        xt_ps = setup_psum.tile([P, PACK, B], BF16, tag="setup")
+        for t in range(PACK):
+            nc.tensor.transpose(xt_ps[:, t, :], x_sb[:, t * P : (t + 1) * P], ident_bf[:])
+        x_grouped = keep.tile([P, B, PACK], BF16, align_bytes=64)
+        nc.vector.tensor_scalar_max(out=x_grouped[:], in0=xt_ps[:].rearrange("p t b -> p b t"), scalar1=0.0)
+
+        bias_ps = setup_psum.tile([P, P], BF16, tag="setup")
+        nc.tensor.transpose(bias_ps[:], bias_rows[:], ident_bf[:])
+        bias_cols = keep.tile([P, 2 * CHUNKS], F32)
+        nc.vector.tensor_copy(out=bias_cols[:], in_=bias_ps[:, 0 : 2 * CHUNKS])
+
+        x_codes = keep.tile([P, B], U32, align_bytes=64)
+        x_scales = keep.tile([P, B], U8, align_bytes=64)
+        quantise(nc, x_grouped[:], x_codes[:], x_scales[:])
+
+        w1_codes = keep.tile([P, DO], U32, align_bytes=64)
+        w1_scales = keep.tile([P, DO], U8, align_bytes=64)
+        w1_grouped = []
+        for half in range(HALVES):
+            w1_grouped.append(regroup_weights(nc, stage, w1_raw[:, :, half * BANK : (half + 1) * BANK]))
+        h_banks = []
+        for half in range(HALVES):
+            cols = slice(half * BANK, (half + 1) * BANK)
+            quantise(nc, w1_grouped[half][:], w1_codes[:, cols], w1_scales[:, cols])
+            h_ps = setup_psum.tile([P, CHUNKS_PER_BANK, B], F32, tag="setup")
+            for q in range(CHUNKS_PER_BANK):
+                m = half * CHUNKS_PER_BANK + q
+                nc.tensor.matmul_mx(
+                    out=h_ps[:, q, :],
+                    lhsT=w1_codes[:, m * P : (m + 1) * P].bitcast(FP8X4),
+                    lhsT_scale=w1_scales[:, m * P : (m + 1) * P],
+                    rhs=x_codes[:].bitcast(FP8X4),
+                    rhs_scale=x_scales[:],
+                    start=True,
+                    stop=True,
+                )
+            h_banks.append(h_ps)
+
+        w2_codes = keep.tile([P, PASSES2, DO], U32, align_bytes=64)
+        w2_scales = keep.tile([P, PASSES2, DO], U8, align_bytes=64)
+        w2_pieces = [(half, g) for half in range(HALVES) for g in range(PASSES2)]
+
+        def regroup_w2_piece(piece):
+            half, g = piece
+            return regroup_weights(nc, stage, w2_raw[:, g, :, half * BANK : (half + 1) * BANK])
+
+        w2_grouped = [regroup_w2_piece(w2_pieces[0])]
+
+        h_rows = keep.tile([P, PASSES2, PACK, B], BF16)
+        for t in range(PACK):
+            nc.scalar.activation(
+                out=h_rows[:, 0, t, :], in_=h_banks[0][:, t, :], func=ACT.Relu, bias=bias_cols[:, t : t + 1], scale=1.0
+            )
+        for t in range(PACK):
+            nc.vector.tensor_scalar(
+                out=h_rows[:, 1, t, :],
+                in0=h_banks[1][:, t, :],
+                scalar1=bias_cols[:, PACK + t : PACK + t + 1],
+                scalar2=0.0,
+                op0=ALU.add,
+                op1=ALU.max,
+            )
+        h_grouped = keep.tile([P, PASSES2, B, PACK], BF16, align_bytes=64)
+        nc.vector.tensor_copy(out=h_grouped[:], in_=h_rows[:].rearrange("p g t b -> p g b t"))
+        w2_grouped.append(regroup_w2_piece(w2_pieces[1]))
+        h_codes = keep.tile([P, PASSES2, B], U32, align_bytes=64)
+        h_scales = keep.tile([P, PASSES2, B], U8, align_bytes=64)
+        quantise(
+            nc,
+            h_grouped[:].rearrange("p g b t -> p (g b) t"),
+            h_codes[:].rearrange("p g b -> p (g b)"),
+            h_scales[:].rearrange("p g b -> p (g b)"),
+        )
+        for index in range(len(w2_pieces)):
+            half, g = w2_pieces[index]
+            cols = slice(half * BANK, (half + 1) * BANK)
+            quantise(nc, w2_grouped[index][:], w2_codes[:, g, cols], w2_scales[:, g, cols])
+            if index + 2 < len(w2_pieces):
+                w2_grouped.append(regroup_w2_piece(w2_pieces[index + 2]))
+
+        label_ps = setup_psum.tile([P, CHUNKS, L], BF16, tag="setup")
+        for c in range(CHUNKS):
+            nc.tensor.transpose(label_ps[:, c, :], label_sb[:, c * P : (c + 1) * P], ident_bf[:])
+        label_t = keep.tile([P, CHUNKS, L], F32)
+        nc.scalar.copy(out=label_t[:], in_=label_ps[:])
+
+        emb_t = keep.tile([P, CHUNKS, B], F32)
+        e_banks = []
+        for half in range(HALVES):
+            e_ps = setup_psum.tile([P, CHUNKS_PER_BANK, B], F32, tag="setup")
+            for q in range(CHUNKS_PER_BANK):
+                c = half * CHUNKS_PER_BANK + q
+                for g in range(PASSES2):
+                    nc.tensor.matmul_mx(
+                        out=e_ps[:, q, :],
+                        lhsT=w2_codes[:, g, c * P : (c + 1) * P].bitcast(FP8X4),
+                        lhsT_scale=w2_scales[:, g, c * P : (c + 1) * P],
+                        rhs=h_codes[:, g, :].bitcast(FP8X4),
+                        rhs_scale=h_scales[:, g, :],
+                        start=(g == 0),
+                        stop=(g == PASSES2 - 1),
+                    )
+            e_banks.append(e_ps)
+        for half in range(HALVES):
+            for q in range(CHUNKS_PER_BANK):
+                c = half * CHUNKS_PER_BANK + q
+                nc.scalar.activation(
+                    out=emb_t[:, c, :],
+                    in_=e_banks[half][:, q, :],
+                    func=ACT.Identity,
+                    bias=bias_cols[:, CHUNKS + c : CHUNKS + c + 1],
+                    scale=1.0,
+                )
+
+        square_sums = keep.tile([P, HALVES, FIRST_WAY_LABELS], F32)
+        total = keep.tile([P, L], F32)
+
+        def first_way(l):
+            for half in range(HALVES):
+                neg_relu = work.tile([P, BANK], F32)
+                flipped = score_psum.tile([P, BANK], F32)
+                for q in range(CHUNKS_PER_BANK):
+                    c = half * CHUNKS_PER_BANK + q
+                    cols = slice(q * P, (q + 1) * P)
+                    nc.vector.tensor_scalar(
+                        out=neg_relu[:, cols],
+                        in0=emb_t[:, c, :],
+                        scalar1=label_t[:, c, l : l + 1],
+                        scalar2=0.0,
+                        op0=ALU.subtract,
+                        op1=ALU.min,
+                    )
+                    nc.tensor.transpose(flipped[:, cols], neg_relu[:, cols], ident_f32[:])
+                squares = work.tile([P, BANK], F32)
+                nc.scalar.activation(
+                    out=squares[:], in_=flipped[:], func=ACT.Square, accum_out=square_sums[:, half, l : l + 1]
+                )
+
+        emb_rows = keep.tile([P, DO], F32)
+        rows_banks = {}
+        diffs = {}
+
+        def flip_emb_back(half):
+            rows_ps = setup_psum.tile([P, BANK], F32, tag="setup")
+            for q in range(CHUNKS_PER_BANK):
+                c = half * CHUNKS_PER_BANK + q
+                nc.tensor.transpose(rows_ps[:, q * P : (q + 1) * P], emb_t[:, c, :], ident_f32[:])
+            rows_banks[half] = rows_ps
+
+        def keep_emb_rows(half):
+            nc.vector.tensor_copy(out=emb_rows[:, half * BANK : (half + 1) * BANK], in_=rows_banks[half][:])
+
+        def difference(i):
+            diff = wide.tile([P, DO], F32)
+            nc.vector.tensor_sub(out=diff[:], in0=label_bcast[:, i, :], in1=emb_rows[:])
+            diffs[i] = diff
+
+        def sum_of_squares(i):
+            products = wide.tile([P, DO], F32)
+            nc.vector.scalar_tensor_tensor(
+                out=products[:],
+                in0=diffs[i][:],
+                scalar=0.0,
+                in1=diffs[i][:],
+                op0=ALU.max,
+                op1=ALU.mult,
+                accum_out=total[:, FIRST_WAY_LABELS + i : FIRST_WAY_LABELS + i + 1],
+            )
+
+        second_way_steps = [(flip_emb_back, half) for half in range(HALVES)]
+        second_way_steps.extend([(keep_emb_rows, half) for half in range(HALVES)])
+        for i in range(SECOND_WAY_LABELS):
+            second_way_steps.append((difference, i))
+            second_way_steps.append((sum_of_squares, i))
+
+        steps_done = 0
+        for l in range(FIRST_WAY_LABELS):
+            first_way(l)
+            while steps_done * FIRST_WAY_LABELS < (l + 1) * len(second_way_steps):
+                step, argument = second_way_steps[steps_done]
+                step(argument)
+                steps_done += 1
+
+        nc.vector.tensor_add(out=total[:, 0:FIRST_WAY_LABELS], in0=square_sums[:, 0, :], in1=square_sums[:, 1, :])
+        nc.scalar.activation(out=total[:], in_=total[:], func=ACT.Sqrt, bias=SQRT_GUARD, scale=1.0)
+        scores = keep.tile([P, L], F32)
+        nc.vector.tensor_scalar_mul(out=scores[:], in0=total[:], scalar1=-1.0)
+        nc.sync.dma_start(out=out, in_=scores[:])

@@ -22,9 +22,12 @@ BANK = 512
 CHUNKS_PER_BANK = BANK // P
 HALVES = CHUNKS // CHUNKS_PER_BANK
 RUN = 4
-SECOND_WAY_LABELS = 22
-FIRST_WAY_LABELS = L - SECOND_WAY_LABELS
-LABELS_PER_BROADCAST = 2
+BANKS = L * HALVES
+VECTOR_EVERY = 5
+VECTOR_FIRST = 3
+VECTOR_BANKS = len(range(VECTOR_FIRST, BANKS, VECTOR_EVERY))
+READ_LAG = 2
+BN_STATS = 6
 SQRT_GUARD = 1e-30
 
 FLOPS = 2 * B * K1 * DO + 2 * B * DO * DO + 4 * B * L * DO
@@ -50,10 +53,8 @@ def tile_relationembedding_s_kernel(tc, sbj_vec, obj_vec, W1, b1, W2, b2, label_
         ctx.enter_context(tc.manual_schedule())
         keep = ctx.enter_context(tc.tile_pool(name="keep", bufs=1))
         stage = ctx.enter_context(tc.tile_pool(name="stage", bufs=3))
-        work = ctx.enter_context(tc.tile_pool(name="work", bufs=6))
-        wide = ctx.enter_context(tc.tile_pool(name="wide", bufs=2))
-        setup_psum = ctx.enter_context(tc.psum_pool(name="setup_psum", bufs=3))
-        score_psum = ctx.enter_context(tc.psum_pool(name="score_psum", bufs=5))
+        work = ctx.enter_context(tc.tile_pool(name="work", bufs=8))
+        psum = ctx.enter_context(tc.psum_pool(name="psum", bufs=8))
 
         x_sb = keep.tile([P, K1], BF16)
         nc.sync.dma_start(out=x_sb[:, 0:DH], in_=sbj_vec)
@@ -75,13 +76,6 @@ def tile_relationembedding_s_kernel(tc, sbj_vec, obj_vec, W1, b1, W2, b2, label_
                 nc.sync.dma_start(out=w2_raw[:, g, :, cols], in_=w2_view[:, g, :, cols])
         label_sb = keep.tile([P, DO], BF16)
         nc.sync.dma_start(out=label_sb[:], in_=label_vecs)
-        label_bcast = keep.tile([P, SECOND_WAY_LABELS, DO], BF16)
-        for i0 in range(0, SECOND_WAY_LABELS, LABELS_PER_BROADCAST):
-            own_rows = label_vecs[FIRST_WAY_LABELS + i0 : FIRST_WAY_LABELS + i0 + LABELS_PER_BROADCAST, :]
-            nc.sync.dma_start(
-                out=label_bcast[:, i0 : i0 + LABELS_PER_BROADCAST, :].rearrange("p l d -> p (l d)"),
-                in_=own_rows.rearrange("l d -> (l d)").partition_broadcast(P),
-            )
 
         ident_bf = keep.tile([P, P], BF16)
         make_identity(nc, ident_bf[:])
@@ -91,13 +85,13 @@ def tile_relationembedding_s_kernel(tc, sbj_vec, obj_vec, W1, b1, W2, b2, label_
         nc.vector.memset(one[:], 1.0)
         nc.scalar.sqrt(out=one[:], in_=one[:])
 
-        xt_ps = setup_psum.tile([P, PACK, B], BF16, tag="setup")
+        xt_ps = psum.tile([P, PACK, B], BF16, tag="bank")
         for t in range(PACK):
             nc.tensor.transpose(xt_ps[:, t, :], x_sb[:, t * P : (t + 1) * P], ident_bf[:])
         x_grouped = keep.tile([P, B, PACK], BF16, align_bytes=64)
         nc.vector.tensor_scalar_max(out=x_grouped[:], in0=xt_ps[:].rearrange("p t b -> p b t"), scalar1=0.0)
 
-        bias_ps = setup_psum.tile([P, P], BF16, tag="setup")
+        bias_ps = psum.tile([P, P], BF16, tag="bank")
         nc.tensor.transpose(bias_ps[:], bias_rows[:], ident_bf[:])
         bias_cols = keep.tile([P, 2 * CHUNKS], F32)
         nc.vector.tensor_copy(out=bias_cols[:], in_=bias_ps[:, 0 : 2 * CHUNKS])
@@ -115,7 +109,7 @@ def tile_relationembedding_s_kernel(tc, sbj_vec, obj_vec, W1, b1, W2, b2, label_
         for half in range(HALVES):
             cols = slice(half * BANK, (half + 1) * BANK)
             quantise(nc, w1_grouped[half][:], w1_codes[:, cols], w1_scales[:, cols])
-            h_ps = setup_psum.tile([P, CHUNKS_PER_BANK, B], F32, tag="setup")
+            h_ps = psum.tile([P, CHUNKS_PER_BANK, B], F32, tag="bank")
             for q in range(CHUNKS_PER_BANK):
                 m = half * CHUNKS_PER_BANK + q
                 nc.tensor.matmul_mx(
@@ -171,7 +165,7 @@ def tile_relationembedding_s_kernel(tc, sbj_vec, obj_vec, W1, b1, W2, b2, label_
             if index + 2 < len(w2_pieces):
                 w2_grouped.append(regroup_w2_piece(w2_pieces[index + 2]))
 
-        label_ps = setup_psum.tile([P, CHUNKS, L], BF16, tag="setup")
+        label_ps = psum.tile([P, CHUNKS, L], BF16, tag="bank")
         for c in range(CHUNKS):
             nc.tensor.transpose(label_ps[:, c, :], label_sb[:, c * P : (c + 1) * P], ident_bf[:])
         label_t = keep.tile([P, CHUNKS, L], F32)
@@ -180,7 +174,7 @@ def tile_relationembedding_s_kernel(tc, sbj_vec, obj_vec, W1, b1, W2, b2, label_
         emb_t = keep.tile([P, CHUNKS, B], F32)
         e_banks = []
         for half in range(HALVES):
-            e_ps = setup_psum.tile([P, CHUNKS_PER_BANK, B], F32, tag="setup")
+            e_ps = psum.tile([P, CHUNKS_PER_BANK, B], F32, tag="bank")
             for q in range(CHUNKS_PER_BANK):
                 c = half * CHUNKS_PER_BANK + q
                 for g in range(PASSES2):
@@ -205,76 +199,59 @@ def tile_relationembedding_s_kernel(tc, sbj_vec, obj_vec, W1, b1, W2, b2, label_
                     scale=1.0,
                 )
 
-        square_sums = keep.tile([P, HALVES, FIRST_WAY_LABELS], F32)
-        total = keep.tile([P, L], F32)
+        square_sums = keep.tile([P, BANKS], F32)
+        stats = keep.tile([P, VECTOR_BANKS, BN_STATS], F32)
+        vector_banks = {}
 
-        def first_way(l):
-            for half in range(HALVES):
-                neg_relu = work.tile([P, BANK], F32)
-                flipped = score_psum.tile([P, BANK], F32)
-                for q in range(CHUNKS_PER_BANK):
-                    c = half * CHUNKS_PER_BANK + q
-                    cols = slice(q * P, (q + 1) * P)
-                    nc.vector.tensor_scalar(
-                        out=neg_relu[:, cols],
-                        in0=emb_t[:, c, :],
-                        scalar1=label_t[:, c, l : l + 1],
-                        scalar2=0.0,
-                        op0=ALU.subtract,
-                        op1=ALU.min,
-                    )
-                    nc.tensor.transpose(flipped[:, cols], neg_relu[:, cols], ident_f32[:])
-                squares = work.tile([P, BANK], F32)
-                nc.scalar.activation(
-                    out=squares[:], in_=flipped[:], func=ACT.Square, accum_out=square_sums[:, half, l : l + 1]
-                )
-
-        emb_rows = keep.tile([P, DO], F32)
-        rows_banks = {}
-        diffs = {}
-
-        def flip_emb_back(half):
-            rows_ps = setup_psum.tile([P, BANK], F32, tag="setup")
+        def fill_bank(k):
+            l, half = divmod(k, HALVES)
+            neg_relu = work.tile([P, BANK], F32)
+            flipped = psum.tile([P, BANK], F32, tag="bank")
             for q in range(CHUNKS_PER_BANK):
                 c = half * CHUNKS_PER_BANK + q
-                nc.tensor.transpose(rows_ps[:, q * P : (q + 1) * P], emb_t[:, c, :], ident_f32[:])
-            rows_banks[half] = rows_ps
+                cols = slice(q * P, (q + 1) * P)
+                nc.vector.tensor_scalar(
+                    out=neg_relu[:, cols],
+                    in0=emb_t[:, c, :],
+                    scalar1=label_t[:, c, l : l + 1],
+                    scalar2=0.0,
+                    op0=ALU.subtract,
+                    op1=ALU.min,
+                )
+                nc.tensor.transpose(flipped[:, cols], neg_relu[:, cols], ident_f32[:])
+            if k % VECTOR_EVERY == VECTOR_FIRST:
+                vector_banks[k] = flipped
+            else:
+                squares = work.tile([P, BANK], F32)
+                nc.scalar.activation(
+                    out=squares[:], in_=flipped[:], func=ACT.Square, accum_out=square_sums[:, k : k + 1]
+                )
 
-        def keep_emb_rows(half):
-            nc.vector.tensor_copy(out=emb_rows[:, half * BANK : (half + 1) * BANK], in_=rows_banks[half][:])
+        for k in range(BANKS + READ_LAG):
+            if k < BANKS:
+                fill_bank(k)
+            ready = k - READ_LAG
+            if ready in vector_banks:
+                nc.vector.bn_stats(out=stats[:, ready // VECTOR_EVERY, :], in_=vector_banks[ready][:])
 
-        def difference(i):
-            diff = wide.tile([P, DO], F32)
-            nc.vector.tensor_sub(out=diff[:], in0=label_bcast[:, i, :], in1=emb_rows[:])
-            diffs[i] = diff
+        by_parity = stats[:].rearrange("p n (e s) -> p n e s", e=2)
+        energy = keep.tile([P, VECTOR_BANKS, 2], F32)
+        nc.vector.tensor_mul(out=energy[:], in0=by_parity[:, :, :, 1], in1=by_parity[:, :, :, 1])
+        nc.vector.scalar_tensor_tensor(
+            out=energy[:],
+            in0=energy[:],
+            scalar=BANK / 2,
+            in1=by_parity[:, :, :, 2],
+            op0=ALU.mult,
+            op1=ALU.add,
+        )
+        nc.vector.tensor_add(
+            out=square_sums[:, VECTOR_FIRST:BANKS:VECTOR_EVERY], in0=energy[:, :, 0], in1=energy[:, :, 1]
+        )
 
-        def sum_of_squares(i):
-            products = wide.tile([P, DO], F32)
-            nc.vector.scalar_tensor_tensor(
-                out=products[:],
-                in0=diffs[i][:],
-                scalar=0.0,
-                in1=diffs[i][:],
-                op0=ALU.max,
-                op1=ALU.mult,
-                accum_out=total[:, FIRST_WAY_LABELS + i : FIRST_WAY_LABELS + i + 1],
-            )
-
-        second_way_steps = [(flip_emb_back, half) for half in range(HALVES)]
-        second_way_steps.extend([(keep_emb_rows, half) for half in range(HALVES)])
-        for i in range(SECOND_WAY_LABELS):
-            second_way_steps.append((difference, i))
-            second_way_steps.append((sum_of_squares, i))
-
-        steps_done = 0
-        for l in range(FIRST_WAY_LABELS):
-            first_way(l)
-            while steps_done * FIRST_WAY_LABELS < (l + 1) * len(second_way_steps):
-                step, argument = second_way_steps[steps_done]
-                step(argument)
-                steps_done += 1
-
-        nc.vector.tensor_add(out=total[:, 0:FIRST_WAY_LABELS], in0=square_sums[:, 0, :], in1=square_sums[:, 1, :])
+        total = keep.tile([P, L], F32)
+        by_half = square_sums[:].rearrange("p (l h) -> p l h", h=HALVES)
+        nc.vector.tensor_add(out=total[:], in0=by_half[:, :, 0], in1=by_half[:, :, 1])
         nc.scalar.activation(out=total[:], in_=total[:], func=ACT.Sqrt, bias=SQRT_GUARD, scale=1.0)
         scores = keep.tile([P, L], F32)
         nc.vector.tensor_scalar_mul(out=scores[:], in0=total[:], scalar1=-1.0)

@@ -27,6 +27,7 @@ VECTOR_EVERY = 5
 VECTOR_FIRST = 3
 VECTOR_BANKS = len(range(VECTOR_FIRST, BANKS, VECTOR_EVERY))
 READ_LAG = 2
+CLOCK_EVERY = 4
 BN_STATS = 6
 SQRT_GUARD = 1e-30
 
@@ -54,7 +55,8 @@ def tile_relationembedding_s_kernel(tc, sbj_vec, obj_vec, W1, b1, W2, b2, label_
         keep = ctx.enter_context(tc.tile_pool(name="keep", bufs=1))
         stage = ctx.enter_context(tc.tile_pool(name="stage", bufs=3))
         work = ctx.enter_context(tc.tile_pool(name="work", bufs=8))
-        psum = ctx.enter_context(tc.psum_pool(name="psum", bufs=8))
+        psum = ctx.enter_context(tc.psum_pool(name="psum", bufs=7))
+        clock_psum = ctx.enter_context(tc.psum_pool(name="clock_psum", bufs=1))
 
         x_sb = keep.tile([P, K1], BF16)
         nc.sync.dma_start(out=x_sb[:, 0:DH], in_=sbj_vec)
@@ -227,9 +229,20 @@ def tile_relationembedding_s_kernel(tc, sbj_vec, obj_vec, W1, b1, W2, b2, label_
                     out=squares[:], in_=flipped[:], func=ACT.Square, accum_out=square_sums[:, k : k + 1]
                 )
 
+        unread = clock_psum.tile([P, BANK], F32)
         for k in range(BANKS + READ_LAG):
             if k < BANKS:
                 fill_bank(k)
+                if k % CLOCK_EVERY == 0:
+                    nc.tensor.matmul_mx(
+                        out=unread[:],
+                        lhsT=x_codes[:].bitcast(FP8X4),
+                        lhsT_scale=x_scales[:],
+                        rhs=w1_codes[:, 0:BANK].bitcast(FP8X4),
+                        rhs_scale=w1_scales[:, 0:BANK],
+                        start=True,
+                        stop=True,
+                    )
             ready = k - READ_LAG
             if ready in vector_banks:
                 nc.vector.bn_stats(out=stats[:, ready // VECTOR_EVERY, :], in_=vector_banks[ready][:])

@@ -26,7 +26,9 @@ BANKS = L * HALVES
 VECTOR_EVERY = 5
 VECTOR_FIRST = 3
 VECTOR_BANKS = len(range(VECTOR_FIRST, BANKS, VECTOR_EVERY))
-READ_LAG = 2
+READ_LAG = 4
+VECTOR_COLS = 320
+STEP_EVERY = 2
 CLOCK_EVERY = 4
 BN_STATS = 6
 SQRT_GUARD = 1e-30
@@ -38,9 +40,9 @@ def regroup_weights(nc, stage, raw):
     grouped = stage.tile([P, BANK, PACK], BF16, align_bytes=64)
     dst = grouped[:].rearrange("p (c i) t -> p c t i", i=RUN)
     src = raw.rearrange("p t (c i) -> p c t i", i=RUN)
-    runs = BANK // RUN
-    nc.vector.tensor_copy(out=dst[:, 0 : runs // 2], in_=src[:, 0 : runs // 2])
-    nc.scalar.copy(out=dst[:, runs // 2 : runs], in_=src[:, runs // 2 : runs])
+    cut = VECTOR_COLS // RUN
+    nc.vector.tensor_copy(out=dst[:, 0:cut], in_=src[:, 0:cut])
+    nc.scalar.copy(out=dst[:, cut:], in_=src[:, cut:])
     return grouped
 
 
@@ -61,23 +63,24 @@ def tile_relationembedding_s_kernel(tc, sbj_vec, obj_vec, W1, b1, W2, b2, label_
         x_sb = keep.tile([P, K1], BF16)
         nc.sync.dma_start(out=x_sb[:, 0:DH], in_=sbj_vec)
         nc.sync.dma_start(out=x_sb[:, DH:K1], in_=obj_vec)
-        bias_rows = keep.tile([P, P], BF16)
-        nc.vector.memset(bias_rows[:], 0.0)
-        nc.sync.dma_start(out=bias_rows[0:CHUNKS, :], in_=b1.rearrange("(m p) -> m p", p=P))
-        nc.sync.dma_start(out=bias_rows[CHUNKS : 2 * CHUNKS, :], in_=b2.rearrange("(m p) -> m p", p=P))
         w1_raw = keep.tile([P, PACK, DO], BF16)
         w1_view = W1.rearrange("(t p) n -> p t n", p=P)
         for half in range(HALVES):
             cols = slice(half * BANK, (half + 1) * BANK)
             nc.sync.dma_start(out=w1_raw[:, :, cols], in_=w1_view[:, :, cols])
+        bias_rows = keep.tile([P, P], BF16)
+        nc.vector.memset(bias_rows[:], 0.0)
+        nc.sync.dma_start(out=bias_rows[0:CHUNKS, :], in_=b1.rearrange("(m p) -> m p", p=P))
+        nc.sync.dma_start(out=bias_rows[CHUNKS : 2 * CHUNKS, :], in_=b2.rearrange("(m p) -> m p", p=P))
         w2_raw = keep.tile([P, PASSES2, PACK, DO], BF16)
         w2_view = W2.rearrange("(g t p) n -> p g t n", t=PACK, p=P)
+        label_sb = keep.tile([P, DO], BF16)
         for half in range(HALVES):
             cols = slice(half * BANK, (half + 1) * BANK)
             for g in range(PASSES2):
                 nc.sync.dma_start(out=w2_raw[:, g, :, cols], in_=w2_view[:, g, :, cols])
-        label_sb = keep.tile([P, DO], BF16)
-        nc.sync.dma_start(out=label_sb[:], in_=label_vecs)
+            if half == 0:
+                nc.sync.dma_start(out=label_sb[:], in_=label_vecs)
 
         ident_bf = keep.tile([P, P], BF16)
         make_identity(nc, ident_bf[:])
@@ -93,24 +96,31 @@ def tile_relationembedding_s_kernel(tc, sbj_vec, obj_vec, W1, b1, W2, b2, label_
         x_grouped = keep.tile([P, B, PACK], BF16, align_bytes=64)
         nc.vector.tensor_scalar_max(out=x_grouped[:], in0=xt_ps[:].rearrange("p t b -> p b t"), scalar1=0.0)
 
-        bias_ps = psum.tile([P, P], BF16, tag="bank")
-        nc.tensor.transpose(bias_ps[:], bias_rows[:], ident_bf[:])
-        bias_cols = keep.tile([P, 2 * CHUNKS], F32)
-        nc.vector.tensor_copy(out=bias_cols[:], in_=bias_ps[:, 0 : 2 * CHUNKS])
-
         x_codes = keep.tile([P, B], U32, align_bytes=64)
         x_scales = keep.tile([P, B], U8, align_bytes=64)
-        quantise(nc, x_grouped[:], x_codes[:], x_scales[:])
-
         w1_codes = keep.tile([P, DO], U32, align_bytes=64)
         w1_scales = keep.tile([P, DO], U8, align_bytes=64)
-        w1_grouped = []
-        for half in range(HALVES):
-            w1_grouped.append(regroup_weights(nc, stage, w1_raw[:, :, half * BANK : (half + 1) * BANK]))
-        h_banks = []
-        for half in range(HALVES):
+        w2_codes = keep.tile([P, PASSES2, DO], U32, align_bytes=64)
+        w2_scales = keep.tile([P, PASSES2, DO], U8, align_bytes=64)
+        grouped = {}
+
+        def regroup_w1(half):
+            grouped["w1", half] = regroup_weights(nc, stage, w1_raw[:, :, half * BANK : (half + 1) * BANK])
+
+        def regroup_w2(half, g):
+            grouped["w2", half, g] = regroup_weights(nc, stage, w2_raw[:, g, :, half * BANK : (half + 1) * BANK])
+
+        def quantise_w1(half):
             cols = slice(half * BANK, (half + 1) * BANK)
-            quantise(nc, w1_grouped[half][:], w1_codes[:, cols], w1_scales[:, cols])
+            quantise(nc, grouped["w1", half][:], w1_codes[:, cols], w1_scales[:, cols])
+
+        def quantise_w2(half, g):
+            cols = slice(half * BANK, (half + 1) * BANK)
+            quantise(nc, grouped["w2", half, g][:], w2_codes[:, g, cols], w2_scales[:, g, cols])
+
+        h_banks = {}
+
+        def multiply_hidden(half):
             h_ps = psum.tile([P, CHUNKS_PER_BANK, B], F32, tag="bank")
             for q in range(CHUNKS_PER_BANK):
                 m = half * CHUNKS_PER_BANK + q
@@ -123,17 +133,24 @@ def tile_relationembedding_s_kernel(tc, sbj_vec, obj_vec, W1, b1, W2, b2, label_
                     start=True,
                     stop=True,
                 )
-            h_banks.append(h_ps)
+            h_banks[half] = h_ps
 
-        w2_codes = keep.tile([P, PASSES2, DO], U32, align_bytes=64)
-        w2_scales = keep.tile([P, PASSES2, DO], U8, align_bytes=64)
-        w2_pieces = [(half, g) for half in range(HALVES) for g in range(PASSES2)]
+        regroup_w1(0)
+        quantise(nc, x_grouped[:], x_codes[:], x_scales[:])
+        regroup_w1(1)
+        quantise_w1(0)
+        multiply_hidden(0)
 
-        def regroup_w2_piece(piece):
-            half, g = piece
-            return regroup_weights(nc, stage, w2_raw[:, g, :, half * BANK : (half + 1) * BANK])
+        bias_ps = psum.tile([P, P], BF16, tag="bank")
+        nc.tensor.transpose(bias_ps[:], bias_rows[:], ident_bf[:])
+        bias_cols = keep.tile([P, 2 * CHUNKS], F32)
+        nc.vector.tensor_copy(out=bias_cols[:], in_=bias_ps[:, 0 : 2 * CHUNKS])
+        neg_b2 = keep.tile([P, CHUNKS], F32)
+        nc.vector.tensor_scalar_mul(out=neg_b2[:], in0=bias_cols[:, CHUNKS : 2 * CHUNKS], scalar1=-1.0)
 
-        w2_grouped = [regroup_w2_piece(w2_pieces[0])]
+        quantise_w1(1)
+        multiply_hidden(1)
+        regroup_w2(0, 0)
 
         h_rows = keep.tile([P, PASSES2, PACK, B], BF16)
         for t in range(PACK):
@@ -151,62 +168,76 @@ def tile_relationembedding_s_kernel(tc, sbj_vec, obj_vec, W1, b1, W2, b2, label_
             )
         h_grouped = keep.tile([P, PASSES2, B, PACK], BF16, align_bytes=64)
         nc.vector.tensor_copy(out=h_grouped[:], in_=h_rows[:].rearrange("p g t b -> p g b t"))
-        w2_grouped.append(regroup_w2_piece(w2_pieces[1]))
+        regroup_w2(0, 1)
         h_codes = keep.tile([P, PASSES2, B], U32, align_bytes=64)
         h_scales = keep.tile([P, PASSES2, B], U8, align_bytes=64)
+        quantise_w2(0, 0)
         quantise(
             nc,
             h_grouped[:].rearrange("p g b t -> p (g b) t"),
             h_codes[:].rearrange("p g b -> p (g b)"),
             h_scales[:].rearrange("p g b -> p (g b)"),
         )
-        for index in range(len(w2_pieces)):
-            half, g = w2_pieces[index]
-            cols = slice(half * BANK, (half + 1) * BANK)
-            quantise(nc, w2_grouped[index][:], w2_codes[:, g, cols], w2_scales[:, g, cols])
-            if index + 2 < len(w2_pieces):
-                w2_grouped.append(regroup_w2_piece(w2_pieces[index + 2]))
+        quantise_w2(0, 1)
 
-        label_ps = psum.tile([P, CHUNKS, L], BF16, tag="bank")
-        for c in range(CHUNKS):
-            nc.tensor.transpose(label_ps[:, c, :], label_sb[:, c * P : (c + 1) * P], ident_bf[:])
         label_t = keep.tile([P, CHUNKS, L], F32)
-        nc.scalar.copy(out=label_t[:], in_=label_ps[:])
 
-        emb_t = keep.tile([P, CHUNKS, B], F32)
-        e_banks = []
-        for half in range(HALVES):
-            e_ps = psum.tile([P, CHUNKS_PER_BANK, B], F32, tag="bank")
+        def flip_labels(half):
+            label_ps = psum.tile([P, CHUNKS_PER_BANK, L], BF16, tag="bank")
             for q in range(CHUNKS_PER_BANK):
                 c = half * CHUNKS_PER_BANK + q
-                for g in range(PASSES2):
-                    nc.tensor.matmul_mx(
-                        out=e_ps[:, q, :],
-                        lhsT=w2_codes[:, g, c * P : (c + 1) * P].bitcast(FP8X4),
-                        lhsT_scale=w2_scales[:, g, c * P : (c + 1) * P],
-                        rhs=h_codes[:, g, :].bitcast(FP8X4),
-                        rhs_scale=h_scales[:, g, :],
-                        start=(g == 0),
-                        stop=(g == PASSES2 - 1),
-                    )
-            e_banks.append(e_ps)
-        for half in range(HALVES):
+                nc.tensor.transpose(label_ps[:, q, :], label_sb[:, c * P : (c + 1) * P], ident_bf[:])
             for q in range(CHUNKS_PER_BANK):
                 c = half * CHUNKS_PER_BANK + q
                 nc.scalar.activation(
-                    out=emb_t[:, c, :],
-                    in_=e_banks[half][:, q, :],
-                    func=ACT.Identity,
-                    bias=bias_cols[:, CHUNKS + c : CHUNKS + c + 1],
-                    scale=1.0,
+                    out=label_t[:, c, :], in_=label_ps[:, q, :], func=ACT.Identity, bias=neg_b2[:, c : c + 1], scale=1.0
                 )
+
+        emb_t = keep.tile([P, CHUNKS, B], F32)
+        pair = CHUNKS_PER_BANK // 2
+        e_banks = {}
+
+        def multiply_emb(half):
+            for part in range(2):
+                e_ps = psum.tile([P, pair, B], F32, tag="bank")
+                for q in range(pair):
+                    c = half * CHUNKS_PER_BANK + part * pair + q
+                    for g in range(PASSES2):
+                        nc.tensor.matmul_mx(
+                            out=e_ps[:, q, :],
+                            lhsT=w2_codes[:, g, c * P : (c + 1) * P].bitcast(FP8X4),
+                            lhsT_scale=w2_scales[:, g, c * P : (c + 1) * P],
+                            rhs=h_codes[:, g, :].bitcast(FP8X4),
+                            rhs_scale=h_scales[:, g, :],
+                            start=(g == 0),
+                            stop=(g == PASSES2 - 1),
+                        )
+                e_banks[half, part] = e_ps
+
+        def keep_emb(half):
+            c = half * CHUNKS_PER_BANK
+            nc.vector.tensor_copy(out=emb_t[:, c : c + pair, :], in_=e_banks[half, 0][:])
+            nc.scalar.copy(out=emb_t[:, c + pair : c + 2 * pair, :], in_=e_banks[half, 1][:])
+
+        flip_labels(0)
+        multiply_emb(0)
+        keep_emb(0)
+        second_half_steps = [
+            lambda: regroup_w2(1, 0),
+            lambda: regroup_w2(1, 1),
+            lambda: quantise_w2(1, 0),
+            lambda: flip_labels(1),
+            lambda: quantise_w2(1, 1),
+            lambda: multiply_emb(1),
+            lambda: keep_emb(1),
+        ]
 
         square_sums = keep.tile([P, BANKS], F32)
         stats = keep.tile([P, VECTOR_BANKS, BN_STATS], F32)
         vector_banks = {}
 
         def fill_bank(k):
-            l, half = divmod(k, HALVES)
+            half, l = divmod(k, L)
             neg_relu = work.tile([P, BANK], F32)
             flipped = psum.tile([P, BANK], F32, tag="bank")
             for q in range(CHUNKS_PER_BANK):
@@ -230,22 +261,28 @@ def tile_relationembedding_s_kernel(tc, sbj_vec, obj_vec, W1, b1, W2, b2, label_
                 )
 
         unread = clock_psum.tile([P, BANK], F32)
+
+        def keep_clock():
+            nc.tensor.matmul_mx(
+                out=unread[:],
+                lhsT=x_codes[:].bitcast(FP8X4),
+                lhsT_scale=x_scales[:],
+                rhs=w1_codes[:, 0:BANK].bitcast(FP8X4),
+                rhs_scale=w1_scales[:, 0:BANK],
+                start=True,
+                stop=True,
+            )
+
         for k in range(BANKS + READ_LAG):
             if k < BANKS:
                 fill_bank(k)
                 if k % CLOCK_EVERY == 0:
-                    nc.tensor.matmul_mx(
-                        out=unread[:],
-                        lhsT=x_codes[:].bitcast(FP8X4),
-                        lhsT_scale=x_scales[:],
-                        rhs=w1_codes[:, 0:BANK].bitcast(FP8X4),
-                        rhs_scale=w1_scales[:, 0:BANK],
-                        start=True,
-                        stop=True,
-                    )
+                    keep_clock()
             ready = k - READ_LAG
             if ready in vector_banks:
                 nc.vector.bn_stats(out=stats[:, ready // VECTOR_EVERY, :], in_=vector_banks[ready][:])
+            if k % STEP_EVERY == 1 and k // STEP_EVERY < len(second_half_steps):
+                second_half_steps[k // STEP_EVERY]()
 
         by_parity = stats[:].rearrange("p n (e s) -> p n e s", e=2)
         energy = keep.tile([P, VECTOR_BANKS, 2], F32)
@@ -263,8 +300,7 @@ def tile_relationembedding_s_kernel(tc, sbj_vec, obj_vec, W1, b1, W2, b2, label_
         )
 
         total = keep.tile([P, L], F32)
-        by_half = square_sums[:].rearrange("p (l h) -> p l h", h=HALVES)
-        nc.vector.tensor_add(out=total[:], in0=by_half[:, :, 0], in1=by_half[:, :, 1])
+        nc.vector.tensor_add(out=total[:], in0=square_sums[:, 0:L], in1=square_sums[:, L : 2 * L])
         nc.scalar.activation(out=total[:], in_=total[:], func=ACT.Sqrt, bias=SQRT_GUARD, scale=1.0)
         scores = keep.tile([P, L], F32)
         nc.vector.tensor_scalar_mul(out=scores[:], in0=total[:], scalar1=-1.0)

@@ -23,9 +23,10 @@ CHUNKS_PER_BANK = BANK // P
 HALVES = CHUNKS // CHUNKS_PER_BANK
 RUN = 4
 BANKS = L * HALVES
-VECTOR_EVERY = 5
-VECTOR_FIRST = 3
-VECTOR_BANKS = len(range(VECTOR_FIRST, BANKS, VECTOR_EVERY))
+VECTOR_PERIOD = 14
+VECTOR_PLACES = (4, 9, 13)
+VECTOR_ROUNDS = BANKS // VECTOR_PERIOD
+VECTOR_BANKS = [r * VECTOR_PERIOD + place for r in range(VECTOR_ROUNDS) for place in VECTOR_PLACES]
 READ_LAG = 4
 VECTOR_COLS = 320
 STEP_EVERY = 2
@@ -233,7 +234,7 @@ def tile_relationembedding_s_kernel(tc, sbj_vec, obj_vec, W1, b1, W2, b2, label_
         ]
 
         square_sums = keep.tile([P, BANKS], F32)
-        stats = keep.tile([P, VECTOR_BANKS, BN_STATS], F32)
+        stats = keep.tile([P, len(VECTOR_BANKS), BN_STATS], F32)
         vector_banks = {}
 
         def fill_bank(k):
@@ -252,7 +253,7 @@ def tile_relationembedding_s_kernel(tc, sbj_vec, obj_vec, W1, b1, W2, b2, label_
                     op1=ALU.min,
                 )
                 nc.tensor.transpose(flipped[:, cols], neg_relu[:, cols], ident_f32[:])
-            if k % VECTOR_EVERY == VECTOR_FIRST:
+            if k in VECTOR_BANKS:
                 vector_banks[k] = flipped
             else:
                 squares = work.tile([P, BANK], F32)
@@ -280,12 +281,12 @@ def tile_relationembedding_s_kernel(tc, sbj_vec, obj_vec, W1, b1, W2, b2, label_
                     keep_clock()
             ready = k - READ_LAG
             if ready in vector_banks:
-                nc.vector.bn_stats(out=stats[:, ready // VECTOR_EVERY, :], in_=vector_banks[ready][:])
+                nc.vector.bn_stats(out=stats[:, VECTOR_BANKS.index(ready), :], in_=vector_banks[ready][:])
             if k % STEP_EVERY == 1 and k // STEP_EVERY < len(second_half_steps):
                 second_half_steps[k // STEP_EVERY]()
 
         by_parity = stats[:].rearrange("p n (e s) -> p n e s", e=2)
-        energy = keep.tile([P, VECTOR_BANKS, 2], F32)
+        energy = keep.tile([P, len(VECTOR_BANKS), 2], F32)
         nc.vector.tensor_mul(out=energy[:], in0=by_parity[:, :, :, 1], in1=by_parity[:, :, :, 1])
         nc.vector.scalar_tensor_tensor(
             out=energy[:],
@@ -295,9 +296,13 @@ def tile_relationembedding_s_kernel(tc, sbj_vec, obj_vec, W1, b1, W2, b2, label_
             op0=ALU.mult,
             op1=ALU.add,
         )
-        nc.vector.tensor_add(
-            out=square_sums[:, VECTOR_FIRST:BANKS:VECTOR_EVERY], in0=energy[:, :, 0], in1=energy[:, :, 1]
-        )
+        by_place = energy[:].rearrange("p (r i) e -> p r i e", i=len(VECTOR_PLACES))
+        for i in range(len(VECTOR_PLACES)):
+            nc.vector.tensor_add(
+                out=square_sums[:, VECTOR_PLACES[i] : VECTOR_ROUNDS * VECTOR_PERIOD : VECTOR_PERIOD],
+                in0=by_place[:, :, i, 0],
+                in1=by_place[:, :, i, 1],
+            )
 
         total = keep.tile([P, L], F32)
         nc.vector.tensor_add(out=total[:], in0=square_sums[:, 0:L], in1=square_sums[:, L : 2 * L])

from contextlib import ExitStack

import concourse.mybir as mybir
from concourse.masks import make_identity

BF16 = mybir.dt.bfloat16
F32 = mybir.dt.float32
U32 = mybir.dt.uint32
U8 = mybir.dt.uint8
FP8X4 = mybir.dt.float8_e4m3fn_x4
ALU = mybir.AluOpType
ACT = mybir.ActivationFunctionType

P = 128
PACK = 4
K_PASS = P * PACK
B, DH, DO, L = 128, 256, 1024, 128
K1 = 2 * DH
PASSES2 = DO // K_PASS
CHUNKS = DO // P
BANK = 512
CHUNKS_PER_BANK = BANK // P
HALVES = CHUNKS // CHUNKS_PER_BANK
RUN = 4
BANKS = L * HALVES
VECTOR_PERIOD = 14
VECTOR_PLACES = (4, 9, 13)
VECTOR_ROUNDS = BANKS // VECTOR_PERIOD
VECTOR_BANKS = [r * VECTOR_PERIOD + place for r in range(VECTOR_ROUNDS) for place in VECTOR_PLACES]
READ_LAG = 4
VECTOR_COLS = 320
STEP_EVERY = 2
CLOCK_EVERY = 4
BN_STATS = 6
SQRT_GUARD = 1e-30

FLOPS = 2 * B * K1 * DO + 2 * B * DO * DO + 4 * B * L * DO


def regroup_weights(nc, stage, raw):
    grouped = stage.tile([P, BANK, PACK], BF16, align_bytes=64)
    dst = grouped[:].rearrange("p (c i) t -> p c t i", i=RUN)
    src = raw.rearrange("p t (c i) -> p c t i", i=RUN)
    cut = VECTOR_COLS // RUN
    nc.vector.tensor_copy(out=dst[:, 0:cut], in_=src[:, 0:cut])
    nc.scalar.copy(out=dst[:, cut:], in_=src[:, cut:])
    return grouped


def quantise(nc, grouped, codes, scales):
    nc.vector.quantize_mx(out=codes.bitcast(FP8X4), scales=scales, in_=grouped.rearrange("p n t -> p (n t)"))


def tile_relationembedding_s_kernel(tc, sbj_vec, obj_vec, W1, b1, W2, b2, label_vecs, out):
    nc = tc.nc
    with ExitStack() as ctx:
        ctx.enter_context(tc.manual_schedule())
        keep = ctx.enter_context(tc.tile_pool(name="keep", bufs=1))
        stage = ctx.enter_context(tc.tile_pool(name="stage", bufs=3))
        work = ctx.enter_context(tc.tile_pool(name="work", bufs=8))
        psum = ctx.enter_context(tc.psum_pool(name="psum", bufs=7))
        clock_psum = ctx.enter_context(tc.psum_pool(name="clock_psum", bufs=1))

        x_sb = keep.tile([P, K1], BF16)
        nc.sync.dma_start(out=x_sb[:, 0:DH], in_=sbj_vec)
        nc.sync.dma_start(out=x_sb[:, DH:K1], in_=obj_vec)
        w1_raw = keep.tile([P, PACK, DO], BF16)
        w1_view = W1.rearrange("(t p) n -> p t n", p=P)
        for half in range(HALVES):
            cols = slice(half * BANK, (half + 1) * BANK)
            nc.sync.dma_start(out=w1_raw[:, :, cols], in_=w1_view[:, :, cols])
        bias_rows = keep.tile([P, P], BF16)
        nc.vector.memset(bias_rows[:], 0.0)
        nc.sync.dma_start(out=bias_rows[0:CHUNKS, :], in_=b1.rearrange("(m p) -> m p", p=P))
        nc.sync.dma_start(out=bias_rows[CHUNKS : 2 * CHUNKS, :], in_=b2.rearrange("(m p) -> m p", p=P))
        w2_raw = keep.tile([P, PASSES2, PACK, DO], BF16)
        w2_view = W2.rearrange("(g t p) n -> p g t n", t=PACK, p=P)
        label_sb = keep.tile([P, DO], BF16)
        for half in range(HALVES):
            cols = slice(half * BANK, (half + 1) * BANK)
            for g in range(PASSES2):
                nc.sync.dma_start(out=w2_raw[:, g, :, cols], in_=w2_view[:, g, :, cols])
            if half == 0:
                nc.sync.dma_start(out=label_sb[:], in_=label_vecs)

        ident_bf = keep.tile([P, P], BF16)
        make_identity(nc, ident_bf[:])
        ident_f32 = keep.tile([P, P], F32)
        make_identity(nc, ident_f32[:])
        one = keep.tile([P, 1], F32)
        nc.vector.memset(one[:], 1.0)
        nc.scalar.sqrt(out=one[:], in_=one[:])

        xt_ps = psum.tile([P, PACK, B], BF16, tag="bank")
        for t in range(PACK):
            nc.tensor.transpose(xt_ps[:, t, :], x_sb[:, t * P : (t + 1) * P], ident_bf[:])
        x_grouped = keep.tile([P, B, PACK], BF16, align_bytes=64)
        nc.vector.tensor_scalar_max(out=x_grouped[:], in0=xt_ps[:].rearrange("p t b -> p b t"), scalar1=0.0)

        x_codes = keep.tile([P, B], U32, align_bytes=64)
        x_scales = keep.tile([P, B], U8, align_bytes=64)
        w1_codes = keep.tile([P, DO], U32, align_bytes=64)
        w1_scales = keep.tile([P, DO], U8, align_bytes=64)
        w2_codes = keep.tile([P, PASSES2, DO], U32, align_bytes=64)
        w2_scales = keep.tile([P, PASSES2, DO], U8, align_bytes=64)
        grouped = {}

        def regroup_w1(half):
            grouped["w1", half] = regroup_weights(nc, stage, w1_raw[:, :, half * BANK : (half + 1) * BANK])

        def regroup_w2(half, g):
            grouped["w2", half, g] = regroup_weights(nc, stage, w2_raw[:, g, :, half * BANK : (half + 1) * BANK])

        def quantise_w1(half):
            cols = slice(half * BANK, (half + 1) * BANK)
            quantise(nc, grouped["w1", half][:], w1_codes[:, cols], w1_scales[:, cols])

        def quantise_w2(half, g):
            cols = slice(half * BANK, (half + 1) * BANK)
            quantise(nc, grouped["w2", half, g][:], w2_codes[:, g, cols], w2_scales[:, g, cols])

        h_banks = {}

        def multiply_hidden(half):
            h_ps = psum.tile([P, CHUNKS_PER_BANK, B], F32, tag="bank")
            for q in range(CHUNKS_PER_BANK):
                m = half * CHUNKS_PER_BANK + q
                nc.tensor.matmul_mx(
                    out=h_ps[:, q, :],
                    lhsT=w1_codes[:, m * P : (m + 1) * P].bitcast(FP8X4),
                    lhsT_scale=w1_scales[:, m * P : (m + 1) * P],
                    rhs=x_codes[:].bitcast(FP8X4),
                    rhs_scale=x_scales[:],
                    start=True,
                    stop=True,
                )
            h_banks[half] = h_ps

        regroup_w1(0)
        quantise(nc, x_grouped[:], x_codes[:], x_scales[:])
        regroup_w1(1)
        quantise_w1(0)
        multiply_hidden(0)

        bias_ps = psum.tile([P, P], BF16, tag="bank")
        nc.tensor.transpose(bias_ps[:], bias_rows[:], ident_bf[:])
        bias_cols = keep.tile([P, 2 * CHUNKS], F32)
        nc.vector.tensor_copy(out=bias_cols[:], in_=bias_ps[:, 0 : 2 * CHUNKS])
        neg_b2 = keep.tile([P, CHUNKS], F32)
        nc.vector.tensor_scalar_mul(out=neg_b2[:], in0=bias_cols[:, CHUNKS : 2 * CHUNKS], scalar1=-1.0)

        quantise_w1(1)
        multiply_hidden(1)
        regroup_w2(0, 0)

        h_rows = keep.tile([P, PASSES2, PACK, B], BF16)
        for t in range(PACK):
            nc.scalar.activation(
                out=h_rows[:, 0, t, :], in_=h_banks[0][:, t, :], func=ACT.Relu, bias=bias_cols[:, t : t + 1], scale=1.0
            )
        for t in range(PACK):
            nc.vector.tensor_scalar(
                out=h_rows[:, 1, t, :],
                in0=h_banks[1][:, t, :],
                scalar1=bias_cols[:, PACK + t : PACK + t + 1],
                scalar2=0.0,
                op0=ALU.add,
                op1=ALU.max,
            )
        h_grouped = keep.tile([P, PASSES2, B, PACK], BF16, align_bytes=64)
        nc.vector.tensor_copy(out=h_grouped[:], in_=h_rows[:].rearrange("p g t b -> p g b t"))
        regroup_w2(0, 1)
        h_codes = keep.tile([P, PASSES2, B], U32, align_bytes=64)
        h_scales = keep.tile([P, PASSES2, B], U8, align_bytes=64)
        quantise_w2(0, 0)
        quantise(
            nc,
            h_grouped[:].rearrange("p g b t -> p (g b) t"),
            h_codes[:].rearrange("p g b -> p (g b)"),
            h_scales[:].rearrange("p g b -> p (g b)"),
        )
        quantise_w2(0, 1)

        label_t = keep.tile([P, CHUNKS, L], F32)

        def flip_labels(half):
            label_ps = psum.tile([P, CHUNKS_PER_BANK, L], BF16, tag="bank")
            for q in range(CHUNKS_PER_BANK):
                c = half * CHUNKS_PER_BANK + q
                nc.tensor.transpose(label_ps[:, q, :], label_sb[:, c * P : (c + 1) * P], ident_bf[:])
            for q in range(CHUNKS_PER_BANK):
                c = half * CHUNKS_PER_BANK + q
                nc.scalar.activation(
                    out=label_t[:, c, :], in_=label_ps[:, q, :], func=ACT.Identity, bias=neg_b2[:, c : c + 1], scale=1.0
                )

        emb_t = keep.tile([P, CHUNKS, B], F32)
        pair = CHUNKS_PER_BANK // 2
        e_banks = {}

        def multiply_emb(half):
            for part in range(2):
                e_ps = psum.tile([P, pair, B], F32, tag="bank")
                for q in range(pair):
                    c = half * CHUNKS_PER_BANK + part * pair + q
                    for g in range(PASSES2):
                        nc.tensor.matmul_mx(
                            out=e_ps[:, q, :],
                            lhsT=w2_codes[:, g, c * P : (c + 1) * P].bitcast(FP8X4),
                            lhsT_scale=w2_scales[:, g, c * P : (c + 1) * P],
                            rhs=h_codes[:, g, :].bitcast(FP8X4),
                            rhs_scale=h_scales[:, g, :],
                            start=(g == 0),
                            stop=(g == PASSES2 - 1),
                        )
                e_banks[half, part] = e_ps

        def keep_emb(half):
            c = half * CHUNKS_PER_BANK
            nc.vector.tensor_copy(out=emb_t[:, c : c + pair, :], in_=e_banks[half, 0][:])
            nc.scalar.copy(out=emb_t[:, c + pair : c + 2 * pair, :], in_=e_banks[half, 1][:])

        flip_labels(0)
        multiply_emb(0)
        keep_emb(0)
        second_half_steps = [
            lambda: regroup_w2(1, 0),
            lambda: regroup_w2(1, 1),
            lambda: quantise_w2(1, 0),
            lambda: flip_labels(1),
            lambda: quantise_w2(1, 1),
            lambda: multiply_emb(1),
            lambda: keep_emb(1),
        ]

        square_sums = keep.tile([P, BANKS], F32)
        stats = keep.tile([P, len(VECTOR_BANKS), BN_STATS], F32)
        vector_banks = {}

        def fill_bank(k):
            half, l = divmod(k, L)
            neg_relu = work.tile([P, BANK], F32)
            flipped = psum.tile([P, BANK], F32, tag="bank")
            for q in range(CHUNKS_PER_BANK):
                c = half * CHUNKS_PER_BANK + q
                cols = slice(q * P, (q + 1) * P)
                nc.vector.tensor_scalar(
                    out=neg_relu[:, cols],
                    in0=emb_t[:, c, :],
                    scalar1=label_t[:, c, l : l + 1],
                    scalar2=0.0,
                    op0=ALU.subtract,
                    op1=ALU.min,
                )
                nc.tensor.transpose(flipped[:, cols], neg_relu[:, cols], ident_f32[:])
            if k in VECTOR_BANKS:
                vector_banks[k] = flipped
            else:
                squares = work.tile([P, BANK], F32)
                nc.scalar.activation(
                    out=squares[:], in_=flipped[:], func=ACT.Square, accum_out=square_sums[:, k : k + 1]
                )

        unread = clock_psum.tile([P, BANK], F32)

        def keep_clock():
            nc.tensor.matmul_mx(
                out=unread[:],
                lhsT=x_codes[:].bitcast(FP8X4),
                lhsT_scale=x_scales[:],
                rhs=w1_codes[:, 0:BANK].bitcast(FP8X4),
                rhs_scale=w1_scales[:, 0:BANK],
                start=True,
                stop=True,
            )

        for k in range(BANKS + READ_LAG):
            if k < BANKS:
                fill_bank(k)
                if k % CLOCK_EVERY == 0:
                    keep_clock()
            ready = k - READ_LAG
            if ready in vector_banks:
                nc.vector.bn_stats(out=stats[:, VECTOR_BANKS.index(ready), :], in_=vector_banks[ready][:])
            if k % STEP_EVERY == 1 and k // STEP_EVERY < len(second_half_steps):
                second_half_steps[k // STEP_EVERY]()

        by_parity = stats[:].rearrange("p n (e s) -> p n e s", e=2)
        energy = keep.tile([P, len(VECTOR_BANKS), 2], F32)
        nc.vector.tensor_mul(out=energy[:], in0=by_parity[:, :, :, 1], in1=by_parity[:, :, :, 1])
        nc.vector.scalar_tensor_tensor(
            out=energy[:],
            in0=energy[:],
            scalar=BANK / 2,
            in1=by_parity[:, :, :, 2],
            op0=ALU.mult,
            op1=ALU.add,
        )
        by_place = energy[:].rearrange("p (r i) e -> p r i e", i=len(VECTOR_PLACES))
        for i in range(len(VECTOR_PLACES)):
            nc.vector.tensor_add(
                out=square_sums[:, VECTOR_PLACES[i] : VECTOR_ROUNDS * VECTOR_PERIOD : VECTOR_PERIOD],
                in0=by_place[:, :, i, 0],
                in1=by_place[:, :, i, 1],
            )

        total = keep.tile([P, L], F32)
        nc.vector.tensor_add(out=total[:], in0=square_sums[:, 0:L], in1=square_sums[:, L : 2 * L])
        nc.scalar.activation(out=total[:], in_=total[:], func=ACT.Sqrt, bias=SQRT_GUARD, scale=1.0)
        scores = keep.tile([P, L], F32)
        nc.vector.tensor_scalar_mul(out=scores[:], in0=total[:], scalar1=-1.0)
        nc.sync.dma_start(out=out, in_=scores[:])
